import numpy as np
import ml_dtypes


def mxq(x, axis, fmt="e4m3"):
    dtype, down = {"e4m3": (ml_dtypes.float8_e4m3fn, 7), "e5m2": (ml_dtypes.float8_e5m2, 14)}[fmt]
    v = np.moveaxis(np.asarray(x, np.float32).astype(ml_dtypes.bfloat16).astype(np.float64), axis, -1)
    blocks = v.reshape(v.shape[:-1] + (-1, 32))
    amax = np.abs(blocks).max(-1, keepdims=True)
    byte = np.maximum(np.where(amax > 0, np.frexp(amax)[1] - 1 + 127, 0) - down, 1)
    scale = np.exp2(byte - 127.0)
    codes = (blocks / scale).astype(np.float32).astype(dtype).astype(np.float64)
    return np.moveaxis((codes * scale).reshape(v.shape), -1, axis)


WIDE = False


def mx_kscale(k):
    if not WIDE:
        return np.ones(k)
    levels = np.array([10, -10, 5, -5, 0])
    if k % 512:
        return np.exp2(np.random.permutation(np.resize(levels, k // 32))).repeat(32)
    a = np.empty((k // 512, 16))
    for p in range(k // 512):
        a[p, :8] = np.random.permutation(np.resize(levels, 8))
        for g in range(8):
            far = levels[np.abs(levels - a[p, g]) >= 10]
            a[p, g + 8] = far[np.random.randint(len(far))]
    return np.exp2(a.ravel()).repeat(32)


BF16 = ml_dtypes.bfloat16


def bf(x):
    return np.asarray(x, np.float32).astype(BF16)


def f64(x):
    return np.asarray(x).astype(np.float64)


B, N, G, C_IN, C_OUT, D = 8, 1024, 255, 2, 2, 128
F = (G + 1) * C_IN


def laplacian_with_self_loop(adj):
    m = adj + np.eye(adj.shape[0])
    d = m.sum(1) ** -0.5
    return (m * d[None, :]).T * d[None, :]


def setup_inputs():
    s = mx_kscale(N)
    t = mx_kscale(F)
    a = 0.25 * np.sqrt(N)
    lap = laplacian_with_self_loop(np.random.random_sample((N, N)))
    return {"x": bf(np.random.standard_normal((B, N, C_IN)) * a / s[None, :, None] * t[None, None, :C_IN]),
            "h": bf(np.random.standard_normal((B, N, G * C_IN)) * a / s[None, :, None] * t[None, None, C_IN:]),
            "laplacian": bf(lap * s[None, :]),
            "weights": bf(np.random.standard_normal((G + 1, D, C_IN, C_OUT)) * 3.0 / np.sqrt(F) / t.reshape(G + 1, C_IN)[:, None, :, None]),
            "biases": bf(np.random.standard_normal((D, C_OUT)) * 0.1)}


def reference(x, h, laplacian, weights, biases):
    xh = np.concatenate([f64(x)[:, :, None, :], f64(h).reshape(B, N, G, C_IN)], axis=2)
    ax = mxq(f64(laplacian), 1, "e4m3") @ mxq(xh.reshape(B, N, F), 1, "e4m3")
    w = f64(weights).transpose(0, 2, 1, 3).reshape(F, D * C_OUT)
    out = (mxq(ax, 2, "e4m3") @ mxq(w, 0, "e4m3")) + f64(biases).reshape(D * C_OUT)
    return out.reshape(B, N * D, C_OUT)

@@ -1,0 +1,426 @@
+from contextlib import ExitStack
+
+import concourse.mybir as mybir
+from concourse.masks import make_identity
+
+BF16 = mybir.dt.bfloat16
+F32 = mybir.dt.float32
+U32 = mybir.dt.uint32
+U8 = mybir.dt.uint8
+FP8X4 = mybir.dt.float8_e4m3fn_x4
+ADD = mybir.AluOpType.add
+
+P = 128
+B = 8
+N = 1024
+F = 512
+H = 510
+DO = 256
+G = 2
+PAD = 16
+HP = PAD + 2048
+MT = 8
+NA = 5
+NO = 3
+NH = 2 * B
+WARM = 1
+SBQ = [5, 5, 1, 1, 3, 3, 6, 6, 6, 6, 6, 6, 6, 6, 6, 6]
+GP0 = 6
+MULT = mybir.AluOpType.mult
+
+FLOPS = 2 * B * N * N * F + 2 * B * N * F * DO
+
+
+def tile_tgcngraphconvolution_pa_t_kernel(tc, x, h, laplacian, weights, biases, out):
+    nc = tc.nc
+    with ExitStack() as ctx:
+        const = ctx.enter_context(tc.tile_pool(name="const", bufs=1))
+        hpool = ctx.enter_context(tc.tile_pool(name="hpool", bufs=8))
+        lpool = ctx.enter_context(tc.tile_pool(name="lpool", bufs=4))
+        lgpool = ctx.enter_context(tc.tile_pool(name="lgpool", bufs=4))
+        xpool = ctx.enter_context(tc.tile_pool(name="xpool", bufs=3))
+        xgpool = ctx.enter_context(tc.tile_pool(name="xgpool", bufs=2))
+        apool = ctx.enter_context(tc.tile_pool(name="apool", bufs=4))
+        opool = ctx.enter_context(tc.tile_pool(name="opool", bufs=6))
+        psa = ctx.enter_context(tc.psum_pool(name="psa", bufs=1))
+        pso = ctx.enter_context(tc.psum_pool(name="pso", bufs=1))
+        ctx.enter_context(tc.manual_schedule())
+
+        count = {"a": 0, "o": 0}
+
+        def a_bank():
+            n = count["a"]
+            count["a"] = n + 1
+            return psa.tile([P, 512], F32, tag="a%d" % (n % NA), name="a%d" % (n % NA))
+
+        def o_bank():
+            n = count["o"]
+            count["o"] = n + 1
+            return pso.tile([P, 512], F32, tag="o%d" % (n % NO), name="o%d" % (n % NO))
+
+        h_v = h.rearrange("b (g p j) f -> b g p (j f)", g=G, j=4)
+        x_v = x.rearrange("b (g r) c -> (b g) (r c)", g=G)
+        lap_v = laplacian.rearrange("(r i) n -> r (i n)", i=MT)
+        w_v = weights.rearrange("(a k) d c o -> k a (d c o)", a=2)
+        b_v = biases.rearrange("(a d) o -> a (d o)", a=1)
+        out_v = out.rearrange("b (p r) o -> b p (r o)", p=P)
+
+        xrow = const.tile([P, 1024], BF16, name="xrow")
+        nc.vector.memset(xrow[:], 0.0)
+        nc.scalar.dma_start(out=xrow[0 : G * B, :], in_=x_v)
+        wraw = const.tile([P, 1024], BF16, name="wraw")
+        nc.scalar.dma_start(out=wraw[:].rearrange("k (a r) -> k a r", a=2), in_=w_v)
+        brow = const.tile([P, DO], BF16, name="brow")
+        nc.vector.memset(brow[:], 0.0)
+        nc.scalar.dma_start(out=brow[0:1, :], in_=b_v)
+
+        hraws = []
+        lraws = []
+
+        def load_h(b):
+            hraw = hpool.tile([P, G * HP], BF16, tag="hraw", name="hraw")
+            for g in range(G):
+                nc.gpsimd.memset(hraw[:, HP * g : HP * g + PAD], 0.0)
+                nc.sync.dma_start(
+                    out=hraw[:, HP * g + PAD : HP * g + PAD + 4 * H],
+                    in_=h_v[b][g],
+                )
+            hraws.append(hraw)
+
+        load_h(0)
+        for i2 in range(MT // 2):
+            lraw = lpool.tile([P, 2 * N], BF16, tag="lraw", name="lraw")
+            nc.sync.dma_start(out=lraw[:], in_=lap_v[:, 2 * N * i2 : 2 * N * i2 + 2 * N])
+            lraws.append(lraw)
+        for b in range(1, B):
+            load_h(b)
+
+        ident = const.tile([P, P], F32, name="ident")
+        make_identity(nc, ident[:])
+        perm = const.tile([P, 16 * P], BF16, name="perm")
+        nc.vector.memset(perm[:], 0.0)
+        perm_w = perm[:].rearrange("k (s t q u e) -> k s t q u e", s=4, t=4, q=16, e=2)
+        ident_w = ident[:].rearrange("k (q t u) -> k t q u", q=8, t=4)
+        for a in range(2):
+            for c in range(2):
+                nc.vector.tensor_copy(
+                    out=perm_w[:, 2 * a + c, :, 8 * a : 8 * a + 8, :, c], in_=ident_w
+                )
+        perm_r = perm[:].rearrange("k (s t m) -> k s t m", s=4, t=4)
+        ones = const.tile([P, P], BF16, name="ones")
+        nc.vector.memset(ones[:], 1.0)
+
+        xraw = const.tile([P, B * 16], BF16, name="xraw")
+        xps = a_bank()
+        xw = xrow[:].bitcast(F32).rearrange("q (p j) -> q p j", j=4)
+        for j in range(4):
+            nc.tensor.transpose(xps[:, P * j : P * j + P], xw[:, :, j], ident[:])
+
+        wr = wraw[:].rearrange("k (a d c o) -> k a d c o", a=2, c=2, o=2)
+        gw = const.tile([P, 4 * DO], BF16, name="gw", align_bytes=64)
+        gw_v = gw[:].rearrange("p (n t) -> p n t", t=4)
+        wcodes = const.tile([P, DO], U32, name="wcodes", align_bytes=64)
+        wplane = const.tile([P, DO], U8, name="wplane", align_bytes=64)
+        bias2 = const.tile([P, 512], F32, name="bias2")
+        wpss = []
+        for a in range(2):
+            wps = o_bank()
+            for s in range(2):
+                for n in range(4):
+                    nc.tensor.matmul(
+                        out=wps[:, DO * s : DO * s + DO].rearrange("p (d o) -> p d o", o=2),
+                        lhsT=perm_r[:, n, 2 * a + s, :],
+                        rhs=wr[:, n // 2, :, n % 2, :],
+                        start=(n == 0),
+                        stop=(n == 3),
+                    )
+            wpss.append(wps)
+        bps = o_bank()
+
+        def warm(n):
+            for w in range(n):
+                nc.tensor.matmul(out=bps[:], lhsT=ones[:], rhs=perm[:, 0:512], start=True, stop=True)
+
+        def bias_mm():
+            for s in range(2):
+                nc.tensor.matmul(
+                    out=bps[:, DO * s : DO * s + DO], lhsT=ones[:], rhs=brow[:], start=True, stop=True
+                )
+
+        def wcopy(a):
+            nc.vector.tensor_copy(
+                out=gw_v[:, :, 2 * a : 2 * a + 2],
+                in_=wpss[a][:].rearrange("p (t n) -> p n t", t=2),
+            )
+
+        xv = xraw[:].rearrange("p (b g j c) -> p b g j c", b=B, g=G, j=4)
+        xt = {}
+
+        xgt = {}
+
+        def x_tiles(b):
+            if b not in xt:
+                xcodes = xpool.tile([P, G * F], U32, tag="xcodes", name="xcodes", align_bytes=64)
+                xplane = xpool.tile([P, G * F], U8, tag="xplane", name="xplane", align_bytes=64)
+                xt[b] = (None, xcodes, xplane)
+            return xt[b]
+
+        def xg_tile(q):
+            if q not in xgt:
+                xgt[q] = xgpool.tile([P, F * 4], BF16, tag="xg", name="xg", align_bytes=64)
+            return xgt[q]
+
+        def xg_view(q):
+            return xg_tile(q)[:].rearrange("p (t q e j) -> p t q e j", t=4, q=16, e=8)
+
+        def h_view(q, lo, hi):
+            b, g = q // G, q % G
+            f0 = 32 * lo - 2
+            start = HP * g + PAD
+            if lo == 0:
+                start, f0 = start - 2, 0
+            rows = hraws[b][:, start : start + 4 * H].rearrange("p (j f) -> p j f", j=4)
+            return rows[:, :, f0 : f0 + 32 * (hi - lo)].rearrange(
+                "p j (q t e) -> p t q j e", t=4, e=8
+            )
+
+        def regroup(copy, q, lo, hi):
+            nt = 4 if q < GP0 else 3
+            copy(
+                out=xg_view(q)[:, 0:nt, lo:hi].rearrange("p t q e j -> p t q j e"),
+                in_=h_view(q, lo, hi)[:, 0:nt],
+            )
+
+        def r_scalar_x(q):
+            b, g = q // G, q % G
+            nc.scalar.copy(out=xg_view(q)[:, 0, 0, 0:2, :], in_=xv[:, b, g].rearrange("p j c -> p c j"))
+
+        def r_scalar_h(q):
+            regroup(nc.scalar.copy, q, 0, SBQ[q])
+
+        def r_scalar(q):
+            if q >= NH:
+                return
+            r_scalar_h(q)
+            r_scalar_x(q)
+
+        def r_vector(q):
+            if q >= NH:
+                return
+            regroup(nc.vector.tensor_copy, q, SBQ[q], 16)
+
+        def r_gpsimd(q):
+            if q >= NH or q < GP0:
+                return
+            b, g = q // G, q % G
+            rows = hraws[b][:, HP * g + PAD : HP * g + PAD + 4 * H].rearrange("p (j f) -> p j f", j=4)
+            nc.gpsimd.tensor_scalar(
+                out=xg_view(q)[:, 3],
+                in0=rows[:, :, 22:H].rearrange("p j (k e) -> p k e j", e=8)[:, 0:61:4],
+                scalar1=1.0,
+                scalar2=0.0,
+                op0=MULT,
+                op1=ADD,
+            )
+
+        def q_x(q):
+            if q >= NH:
+                return
+            b, g = q // G, q % G
+            xcodes, xplane = x_tiles(b)[1:]
+            nc.vector.quantize_mx(
+                out=xcodes[:, F * g : F * g + F].bitcast(FP8X4),
+                scales=xplane[:, F * g : F * g + F],
+                in_=xg_tile(q)[:],
+            )
+
+        lcodes = const.tile([P, MT * G * P], U32, name="lcodes", align_bytes=64)
+        lplane = const.tile([P, MT * G * P], U8, name="lplane", align_bytes=64)
+        lgrps = []
+
+        def lap_t(i):
+            lw = lraws[i // 2][:].bitcast(F32)[:, 512 * (i % 2) : 512 * (i % 2) + 512]
+            lps = a_bank()
+            for g in range(G):
+                for u in range(2):
+                    nc.tensor.transpose(
+                        lps[:, P * (2 * g + u) : P * (2 * g + u) + P],
+                        lw[:, 256 * g + u : 256 * g + 256 : 2],
+                        ident[:],
+                    )
+            lgrp = lgpool.tile([P, N], BF16, tag="lgrp", name="lgrp", align_bytes=64)
+            nc.scalar.copy(
+                out=lgrp[:].bitcast(F32).rearrange("p (g m u) -> p g m u", g=G, u=2),
+                in_=lps[:].rearrange("p (g u m) -> p g m u", g=G, u=2),
+            )
+            lgrps.append(lgrp)
+
+        def lap_q(i):
+            nc.vector.quantize_mx(
+                out=lcodes[:, 256 * i : 256 * i + 256].bitcast(FP8X4),
+                scales=lplane[:, 256 * i : 256 * i + 256],
+                in_=lgrps[i][:],
+            )
+
+        at = {}
+
+        def step2(k, tiles):
+            b, hf = k // 2, k % 2
+            xcodes, xplane = x_tiles(b)[1:]
+            if k not in at:
+                ag = apool.tile([P, 2048], BF16, tag="ag", name="ag", align_bytes=64)
+                acodes = apool.tile([P, 512], U32, tag="acodes", name="acodes", align_bytes=64)
+                aplane = apool.tile([P, 512], U8, tag="aplane", name="aplane", align_bytes=64)
+                osb = opool.tile([P, 1024], F32, tag="osb", name="osb")
+                at[k] = (ag, acodes, aplane, osb)
+            ag = at[k][0]
+            for ii in tiles:
+                i = 4 * hf + ii
+                aps = a_bank()
+                for t in range(4):
+                    for g in range(G):
+                        xs = slice(F * g + P * t, F * g + P * t + P)
+                        ls = slice(256 * i + P * g, 256 * i + P * g + P)
+                        nc.tensor.matmul_mx(
+                            out=aps[:, P * t : P * t + P],
+                            lhsT=xcodes[:, xs].bitcast(FP8X4),
+                            lhsT_scale=xplane[:, xs],
+                            rhs=lcodes[:, ls].bitcast(FP8X4),
+                            rhs_scale=lplane[:, ls],
+                            start=(g == 0),
+                            stop=(g == G - 1),
+                        )
+                nc.scalar.copy(
+                    out=ag[:, 512 * ii : 512 * ii + 512].rearrange("p (m t) -> p m t", t=4),
+                    in_=aps[:].rearrange("p (t m) -> p m t", t=4),
+                )
+
+        def q_a(k, lo, hi):
+            ag, acodes, aplane = at[k][0:3]
+            nc.vector.quantize_mx(
+                out=acodes[:, P * lo : P * hi].bitcast(FP8X4),
+                scales=aplane[:, P * lo : P * hi],
+                in_=ag[:, 512 * lo : 512 * hi],
+            )
+
+        def step3(k, pr):
+            acodes, aplane, osb = at[k][1:]
+            ops = o_bank()
+            for s in range(2):
+                cs = slice(P * (2 * pr + s), P * (2 * pr + s) + P)
+                nc.tensor.matmul_mx(
+                    out=ops[:, DO * s : DO * s + DO],
+                    lhsT=acodes[:, cs].bitcast(FP8X4),
+                    lhsT_scale=aplane[:, cs],
+                    rhs=wcodes[:].bitcast(FP8X4),
+                    rhs_scale=wplane[:],
+                    start=True,
+                    stop=True,
+                )
+            nc.vector.tensor_tensor(
+                out=osb[:, 512 * pr : 512 * pr + 512], in0=ops[:], in1=bias2[:], op=ADD
+            )
+
+        def store(k, lo, hi):
+            b, hf = k // 2, k % 2
+            nc.sync.dma_start(
+                out=out_v[b][:, 1024 * hf + 512 * lo : 1024 * hf + 512 * hi],
+                in_=at[k][3][:, 512 * lo : 512 * hi],
+            )
+
+        def step3_tile(k, t):
+            b, hf = k // 2, k % 2
+            acodes, aplane, osb = at[k][1:]
+            ops = o_bank()
+            cs = slice(P * t, P * t + P)
+            nc.tensor.matmul_mx(
+                out=ops[:, 0:DO],
+                lhsT=acodes[:, cs].bitcast(FP8X4),
+                lhsT_scale=aplane[:, cs],
+                rhs=wcodes[:].bitcast(FP8X4),
+                rhs_scale=wplane[:],
+                start=True,
+                stop=True,
+            )
+            nc.vector.tensor_tensor(
+                out=osb[:, DO * t : DO * t + DO], in0=ops[:, 0:DO], in1=bias2[:, 0:DO], op=ADD
+            )
+            nc.sync.dma_start(
+                out=out_v[b][:, 1024 * hf + DO * t : 1024 * hf + DO * t + DO],
+                in_=osb[:, DO * t : DO * t + DO],
+            )
+
+        def step3_all(k):
+            step3(k, 0)
+            step3(k, 1)
+            store(k, 0, 2)
+
+        r_scalar_h(0)
+        r_vector(0)
+        r_scalar_h(1)
+        r_vector(1)
+        nc.scalar.copy(
+            out=xraw[:].bitcast(F32).rearrange("p (q j) -> p q j", j=4),
+            in_=xps[:].rearrange("p (j q) -> p q j", j=4)[:, 0 : G * B, :],
+        )
+        r_scalar_x(0)
+        r_scalar_x(1)
+        wcopy(0)
+        q_x(0)
+        wcopy(1)
+        q_x(1)
+        for i in range(MT):
+            if i % 2 == 0 and i < MT - 2:
+                warm(WARM)
+            if i == MT - 2:
+                bias_mm()
+            lap_t(i)
+        lap_q(0)
+        lap_q(1)
+        nc.vector.quantize_mx(out=wcodes[:].bitcast(FP8X4), scales=wplane[:], in_=gw[:])
+        lap_q(2)
+        lap_q(3)
+        lap_q(4)
+        lap_q(5)
+        r_scalar(2)
+        r_vector(2)
+        lap_q(6)
+        lap_q(7)
+        step2(0, range(0, 2))
+        r_scalar(3)
+        r_vector(3)
+        q_x(2)
+        nc.vector.tensor_copy(out=bias2[:], in_=bps[:])
+
+        for k in range(NH - 2):
+            step2(k, range(2, 4) if k == 0 else range(4))
+            if k >= 2:
+                step3_all(k - 2)
+            r_scalar(k + 4)
+            r_gpsimd(k + 4)
+            q_x(k + 3)
+            q_a(k, 0, 4)
+            r_vector(k + 4)
+
+        k = NH - 2
+        step2(k, range(0, 2))
+        step3_all(k - 2)
+        q_a(k, 0, 2)
+        step2(k, range(2, 4))
+        step3_all(k - 1)
+        q_a(k, 2, 4)
+
+        k = NH - 1
+        step2(k, range(0, 2))
+        step3(k - 1, 0)
+        q_a(k, 0, 2)
+        step2(k, range(2, 3))
+        step3(k - 1, 1)
+        store(k - 1, 0, 2)
+        q_a(k, 2, 3)
+        step2(k, range(3, 4))
+        step3(k, 0)
+        store(k, 0, 1)
+        q_a(k, 3, 4)
+        step3_tile(k, 2)
+        step3_tile(k, 3)

@@ -9,6 +9,7 @@ U32 = mybir.dt.uint32
 U8 = mybir.dt.uint8
 FP8X4 = mybir.dt.float8_e4m3fn_x4
 ADD = mybir.AluOpType.add
+MULT = mybir.AluOpType.mult
 
 P = 128
 B = 8
@@ -23,10 +24,9 @@ MT = 8
 NA = 5
 NO = 3
 NH = 2 * B
-WARM = 1
-SBQ = [5, 5, 1, 1, 3, 3, 6, 6, 6, 6, 6, 6, 6, 6, 6, 6]
-GP0 = 6
-MULT = mybir.AluOpType.mult
+NR = 32
+SR = [16, 16, 4, 4, 8, 8, 16, 16, 16, 16, 16, 16, 16, 16, 16, 16]
+GP0 = 4
 
 FLOPS = 2 * B * N * N * F + 2 * B * N * F * DO
 
@@ -36,10 +36,9 @@ def tile_tgcngraphconvolution_pa_t_kernel(tc, x, h, laplacian, weights, biases, 
     with ExitStack() as ctx:
         const = ctx.enter_context(tc.tile_pool(name="const", bufs=1))
         hpool = ctx.enter_context(tc.tile_pool(name="hpool", bufs=8))
-        lpool = ctx.enter_context(tc.tile_pool(name="lpool", bufs=4))
         lgpool = ctx.enter_context(tc.tile_pool(name="lgpool", bufs=4))
         xpool = ctx.enter_context(tc.tile_pool(name="xpool", bufs=3))
-        xgpool = ctx.enter_context(tc.tile_pool(name="xgpool", bufs=2))
+        xgpool = ctx.enter_context(tc.tile_pool(name="xgpool", bufs=3))
         apool = ctx.enter_context(tc.tile_pool(name="apool", bufs=4))
         opool = ctx.enter_context(tc.tile_pool(name="opool", bufs=6))
         psa = ctx.enter_context(tc.psum_pool(name="psa", bufs=1))
@@ -61,54 +60,52 @@ def tile_tgcngraphconvolution_pa_t_kernel(tc, x, h, laplacian, weights, biases, 
         h_v = h.rearrange("b (g p j) f -> b g p (j f)", g=G, j=4)
         x_v = x.rearrange("b (g r) c -> (b g) (r c)", g=G)
         lap_v = laplacian.rearrange("(r i) n -> r (i n)", i=MT)
-        w_v = weights.rearrange("(a k) d c o -> k a (d c o)", a=2)
+        w_v = weights.rearrange("(r s i) d c o -> s r i (d c o)", s=2, i=4)
         b_v = biases.rearrange("(a d) o -> a (d o)", a=1)
         out_v = out.rearrange("b (p r) o -> b p (r o)", p=P)
 
         xrow = const.tile([P, 1024], BF16, name="xrow")
-        nc.vector.memset(xrow[:], 0.0)
-        nc.scalar.dma_start(out=xrow[0 : G * B, :], in_=x_v)
-        wraw = const.tile([P, 1024], BF16, name="wraw")
-        nc.scalar.dma_start(out=wraw[:].rearrange("k (a r) -> k a r", a=2), in_=w_v)
+        nc.vector.memset(xrow[:].bitcast(F32), 0.0)
         brow = const.tile([P, DO], BF16, name="brow")
-        nc.vector.memset(brow[:], 0.0)
-        nc.scalar.dma_start(out=brow[0:1, :], in_=b_v)
+        nc.vector.memset(brow[:].bitcast(F32), 0.0)
+        wraw = const.tile([P, 1024], BF16, name="wraw")
 
         hraws = []
-        lraws = []
 
-        def load_h(b):
-            hraw = hpool.tile([P, G * HP], BF16, tag="hraw", name="hraw")
-            for g in range(G):
-                nc.gpsimd.memset(hraw[:, HP * g : HP * g + PAD], 0.0)
-                nc.sync.dma_start(
-                    out=hraw[:, HP * g + PAD : HP * g + PAD + 4 * H],
-                    in_=h_v[b][g],
-                )
-            hraws.append(hraw)
+        def load_h(b, g):
+            if g == 0:
+                hraws.append(hpool.tile([P, G * HP], BF16, tag="hraw", name="hraw"))
+            hraw = hraws[b]
+            nc.gpsimd.memset(hraw[:, HP * g : HP * g + PAD], 0.0)
+            nc.sync.dma_start(out=hraw[:, HP * g + PAD : HP * g + PAD + 4 * H], in_=h_v[b][g])
 
-        load_h(0)
-        for i2 in range(MT // 2):
-            lraw = lpool.tile([P, 2 * N], BF16, tag="lraw", name="lraw")
-            nc.sync.dma_start(out=lraw[:], in_=lap_v[:, 2 * N * i2 : 2 * N * i2 + 2 * N])
-            lraws.append(lraw)
+        def load_lap(lo, hi):
+            nc.sync.dma_start(out=lraw[:, N * lo : N * hi], in_=lap_v[:, N * lo : N * hi])
+
+        lraw = const.tile([P, MT * N], BF16, name="lraw")
+
+        load_h(0, 0)
+        nc.sync.dma_start(out=xrow[0 : G * B, :], in_=x_v)
+        nc.sync.dma_start(out=brow[0:1, :], in_=b_v)
+        load_lap(0, 1)
+        load_h(0, 1)
+        load_lap(1, 2)
+        load_lap(2, 3)
+        load_lap(3, 4)
+        load_lap(4, 6)
+        load_lap(6, 8)
+        for s in range(2):
+            nc.sync.dma_start(out=wraw[:, 512 * s : 512 * s + 512], in_=w_v[s])
         for b in range(1, B):
-            load_h(b)
+            load_h(b, 0)
+            load_h(b, 1)
 
         ident = const.tile([P, P], F32, name="ident")
         make_identity(nc, ident[:])
-        perm = const.tile([P, 16 * P], BF16, name="perm")
-        nc.vector.memset(perm[:], 0.0)
-        perm_w = perm[:].rearrange("k (s t q u e) -> k s t q u e", s=4, t=4, q=16, e=2)
-        ident_w = ident[:].rearrange("k (q t u) -> k t q u", q=8, t=4)
-        for a in range(2):
-            for c in range(2):
-                nc.vector.tensor_copy(
-                    out=perm_w[:, 2 * a + c, :, 8 * a : 8 * a + 8, :, c], in_=ident_w
-                )
-        perm_r = perm[:].rearrange("k (s t m) -> k s t m", s=4, t=4)
         ones = const.tile([P, P], BF16, name="ones")
         nc.vector.memset(ones[:], 1.0)
+        warmed = const.tile([P, 1], BF16, name="warmed")
+        nc.scalar.copy(out=warmed[:], in_=ones[:, 0:1])
 
         xraw = const.tile([P, B * 16], BF16, name="xraw")
         xps = a_bank()
@@ -116,30 +113,16 @@ def tile_tgcngraphconvolution_pa_t_kernel(tc, x, h, laplacian, weights, biases, 
         for j in range(4):
             nc.tensor.transpose(xps[:, P * j : P * j + P], xw[:, :, j], ident[:])
 
-        wr = wraw[:].rearrange("k (a d c o) -> k a d c o", a=2, c=2, o=2)
-        gw = const.tile([P, 4 * DO], BF16, name="gw", align_bytes=64)
-        gw_v = gw[:].rearrange("p (n t) -> p n t", t=4)
-        wcodes = const.tile([P, DO], U32, name="wcodes", align_bytes=64)
-        wplane = const.tile([P, DO], U8, name="wplane", align_bytes=64)
-        bias2 = const.tile([P, 512], F32, name="bias2")
-        wpss = []
-        for a in range(2):
-            wps = o_bank()
-            for s in range(2):
-                for n in range(4):
-                    nc.tensor.matmul(
-                        out=wps[:, DO * s : DO * s + DO].rearrange("p (d o) -> p d o", o=2),
-                        lhsT=perm_r[:, n, 2 * a + s, :],
-                        rhs=wr[:, n // 2, :, n % 2, :],
-                        start=(n == 0),
-                        stop=(n == 3),
-                    )
-            wpss.append(wps)
-        bps = o_bank()
+        def x_copy():
+            nc.scalar.copy(
+                out=xraw[:].bitcast(F32).rearrange("p (q j) -> p q j", j=4),
+                in_=xps[:].rearrange("p (j q) -> p q j", j=4)[:, 0 : G * B, :],
+            )
 
-        def warm(n):
-            for w in range(n):
-                nc.tensor.matmul(out=bps[:], lhsT=ones[:], rhs=perm[:, 0:512], start=True, stop=True)
+        xv = xraw[:].rearrange("p (b g j c) -> p b g j c", b=B, g=G, j=4)
+
+        bias2 = const.tile([P, 512], F32, name="bias2")
+        bps = o_bank()
 
         def bias_mm():
             for s in range(2):
@@ -147,22 +130,32 @@ def tile_tgcngraphconvolution_pa_t_kernel(tc, x, h, laplacian, weights, biases, 
                     out=bps[:, DO * s : DO * s + DO], lhsT=ones[:], rhs=brow[:], start=True, stop=True
                 )
 
-        def wcopy(a):
-            nc.vector.tensor_copy(
-                out=gw_v[:, :, 2 * a : 2 * a + 2],
-                in_=wpss[a][:].rearrange("p (t n) -> p n t", t=2),
-            )
+        def bias_copy():
+            nc.vector.tensor_copy(out=bias2[:], in_=bps[:])
 
-        xv = xraw[:].rearrange("p (b g j c) -> p b g j c", b=B, g=G, j=4)
+        gw = const.tile([P, 4 * DO], BF16, name="gw", align_bytes=64)
+        wcodes = const.tile([P, DO], U32, name="wcodes", align_bytes=64)
+        wplane = const.tile([P, DO], U8, name="wplane", align_bytes=64)
+
+        def w_regroup():
+            gw_v = gw[:].rearrange("p (d o s c) -> p s d o c", d=P, o=2, s=2)
+            wr = wraw[:].rearrange("p (s d c o) -> p s d o c", s=2, d=P, c=2)
+            for s in range(2):
+                nc.gpsimd.tensor_scalar(
+                    out=gw_v[:, s], in0=wr[:, s], scalar1=1.0, scalar2=0.0, op0=MULT, op1=ADD
+                )
+
+        def w_q():
+            nc.vector.quantize_mx(out=wcodes[:].bitcast(FP8X4), scales=wplane[:], in_=gw[:])
+
         xt = {}
-
         xgt = {}
 
         def x_tiles(b):
             if b not in xt:
                 xcodes = xpool.tile([P, G * F], U32, tag="xcodes", name="xcodes", align_bytes=64)
                 xplane = xpool.tile([P, G * F], U8, tag="xplane", name="xplane", align_bytes=64)
-                xt[b] = (None, xcodes, xplane)
+                xt[b] = (xcodes, xplane)
             return xt[b]
 
         def xg_tile(q):
@@ -171,75 +164,73 @@ def tile_tgcngraphconvolution_pa_t_kernel(tc, x, h, laplacian, weights, biases, 
             return xgt[q]
 
         def xg_view(q):
-            return xg_tile(q)[:].rearrange("p (t q e j) -> p t q e j", t=4, q=16, e=8)
+            return xg_tile(q)[:].rearrange("p (s c r i j) -> p s c r i j", s=2, c=2, r=NR, i=4)
 
-        def h_view(q, lo, hi):
+        def h_view(q, s, lo, hi):
             b, g = q // G, q % G
-            f0 = 32 * lo - 2
-            start = HP * g + PAD
-            if lo == 0:
-                start, f0 = start - 2, 0
+            start = HP * g + PAD - (2 if s == 0 else 0)
+            f0 = 16 * lo + (0 if s == 0 else 6)
             rows = hraws[b][:, start : start + 4 * H].rearrange("p (j f) -> p j f", j=4)
-            return rows[:, :, f0 : f0 + 32 * (hi - lo)].rearrange(
-                "p j (q t e) -> p t q j e", t=4, e=8
-            )
+            return rows[:, :, f0 : f0 + 16 * (hi - lo) - 8].rearrange(
+                "p j (r i c) -> p c r i j", i=4, c=2
+            )[:, :, 0 : 2 * (hi - lo) - 1 : 2]
 
-        def regroup(copy, q, lo, hi):
-            nt = 4 if q < GP0 else 3
-            copy(
-                out=xg_view(q)[:, 0:nt, lo:hi].rearrange("p t q e j -> p t q j e"),
-                in_=h_view(q, lo, hi)[:, 0:nt],
-            )
+        def regroup(copy, q, s, lo, hi):
+            if lo < hi:
+                copy(
+                    out=xg_view(q)[:, s, :, lo:hi].rearrange("p c r i j -> p c r j i"),
+                    in_=h_view(q, s, lo, hi).rearrange("p c r i j -> p c r j i"),
+                )
 
         def r_scalar_x(q):
-            b, g = q // G, q % G
-            nc.scalar.copy(out=xg_view(q)[:, 0, 0, 0:2, :], in_=xv[:, b, g].rearrange("p j c -> p c j"))
+            if q < NH:
+                b, g = q // G, q % G
+                nc.scalar.copy(
+                    out=xg_view(q)[:, 0, :, 0, 0, :], in_=xv[:, b, g].rearrange("p j c -> p c j")
+                )
 
         def r_scalar_h(q):
-            regroup(nc.scalar.copy, q, 0, SBQ[q])
-
-        def r_scalar(q):
-            if q >= NH:
-                return
-            r_scalar_h(q)
-            r_scalar_x(q)
+            if q < NH:
+                regroup(nc.scalar.copy, q, 0, 0, SR[q])
 
         def r_vector(q):
-            if q >= NH:
-                return
-            regroup(nc.vector.tensor_copy, q, SBQ[q], 16)
+            if q < NH:
+                regroup(nc.vector.tensor_copy, q, 0, SR[q], NR)
+                if q < GP0:
+                    regroup(nc.vector.tensor_copy, q, 1, 0, NR)
+                else:
+                    nc.vector.tensor_copy(
+                        out=xg_view(q)[:, 1, 0].rearrange("p r i j -> p r j i"),
+                        in_=h_view(q, 1, 0, NR)[:, 0].rearrange("p r i j -> p r j i"),
+                    )
 
         def r_gpsimd(q):
-            if q >= NH or q < GP0:
-                return
-            b, g = q // G, q % G
-            rows = hraws[b][:, HP * g + PAD : HP * g + PAD + 4 * H].rearrange("p (j f) -> p j f", j=4)
-            nc.gpsimd.tensor_scalar(
-                out=xg_view(q)[:, 3],
-                in0=rows[:, :, 22:H].rearrange("p j (k e) -> p k e j", e=8)[:, 0:61:4],
-                scalar1=1.0,
-                scalar2=0.0,
-                op0=MULT,
-                op1=ADD,
-            )
+            if GP0 <= q < NH:
+                nc.gpsimd.tensor_scalar(
+                    out=xg_view(q)[:, 1, 1],
+                    in0=h_view(q, 1, 0, NR)[:, 1],
+                    scalar1=1.0,
+                    scalar2=0.0,
+                    op0=MULT,
+                    op1=ADD,
+                )
 
         def q_x(q):
-            if q >= NH:
-                return
-            b, g = q // G, q % G
-            xcodes, xplane = x_tiles(b)[1:]
-            nc.vector.quantize_mx(
-                out=xcodes[:, F * g : F * g + F].bitcast(FP8X4),
-                scales=xplane[:, F * g : F * g + F],
-                in_=xg_tile(q)[:],
-            )
+            if q < NH:
+                b, g = q // G, q % G
+                xcodes, xplane = x_tiles(b)
+                nc.vector.quantize_mx(
+                    out=xcodes[:, F * g : F * g + F].bitcast(FP8X4),
+                    scales=xplane[:, F * g : F * g + F],
+                    in_=xg_tile(q)[:],
+                )
 
         lcodes = const.tile([P, MT * G * P], U32, name="lcodes", align_bytes=64)
         lplane = const.tile([P, MT * G * P], U8, name="lplane", align_bytes=64)
-        lgrps = []
+        lgrps = {}
 
-        def lap_t(i):
-            lw = lraws[i // 2][:].bitcast(F32)[:, 512 * (i % 2) : 512 * (i % 2) + 512]
+        def lap_t(i, copy):
+            lw = lraw[:].bitcast(F32)[:, 512 * i : 512 * i + 512]
             lps = a_bank()
             for g in range(G):
                 for u in range(2):
@@ -249,11 +240,11 @@ def tile_tgcngraphconvolution_pa_t_kernel(tc, x, h, laplacian, weights, biases, 
                         ident[:],
                     )
             lgrp = lgpool.tile([P, N], BF16, tag="lgrp", name="lgrp", align_bytes=64)
-            nc.scalar.copy(
+            copy(
                 out=lgrp[:].bitcast(F32).rearrange("p (g m u) -> p g m u", g=G, u=2),
                 in_=lps[:].rearrange("p (g u m) -> p g m u", g=G, u=2),
             )
-            lgrps.append(lgrp)
+            lgrps[i] = lgrp
 
         def lap_q(i):
             nc.vector.quantize_mx(
@@ -266,7 +257,7 @@ def tile_tgcngraphconvolution_pa_t_kernel(tc, x, h, laplacian, weights, biases, 
 
         def step2(k, tiles):
             b, hf = k // 2, k % 2
-            xcodes, xplane = x_tiles(b)[1:]
+            xcodes, xplane = x_tiles(b)
             if k not in at:
                 ag = apool.tile([P, 2048], BF16, tag="ag", name="ag", align_bytes=64)
                 acodes = apool.tile([P, 512], U32, tag="acodes", name="acodes", align_bytes=64)
@@ -355,48 +346,67 @@ def tile_tgcngraphconvolution_pa_t_kernel(tc, x, h, laplacian, weights, biases, 
             step3(k, 1)
             store(k, 0, 2)
 
-        r_scalar_h(0)
+        on_s, on_v = nc.scalar.copy, nc.vector.tensor_copy
+
         r_vector(0)
-        r_scalar_h(1)
-        r_vector(1)
-        nc.scalar.copy(
-            out=xraw[:].bitcast(F32).rearrange("p (q j) -> p q j", j=4),
-            in_=xps[:].rearrange("p (j q) -> p q j", j=4)[:, 0 : G * B, :],
-        )
+        r_scalar_h(0)
+        x_copy()
         r_scalar_x(0)
-        r_scalar_x(1)
-        wcopy(0)
+        lap_t(0, on_s)
         q_x(0)
-        wcopy(1)
-        q_x(1)
-        for i in range(MT):
-            if i % 2 == 0 and i < MT - 2:
-                warm(WARM)
-            if i == MT - 2:
-                bias_mm()
-            lap_t(i)
+        r_vector(1)
+        r_scalar_h(1)
+        r_scalar_x(1)
         lap_q(0)
+        q_x(1)
+        lap_t(1, on_s)
+        lap_t(2, on_s)
         lap_q(1)
-        nc.vector.quantize_mx(out=wcodes[:].bitcast(FP8X4), scales=wplane[:], in_=gw[:])
+        lap_t(3, on_v)
         lap_q(2)
+        step2(0, range(0, 2))
         lap_q(3)
+        w_regroup()
+        lap_t(4, on_s)
+        lap_t(5, on_s)
+        step2(0, range(2, 4))
         lap_q(4)
-        lap_q(5)
-        r_scalar(2)
         r_vector(2)
+        r_scalar_h(2)
+        r_scalar_x(2)
+        lap_q(5)
+        lap_t(6, on_s)
+        lap_t(7, on_s)
+        bias_mm()
+        step2(1, range(0, 2))
+        r_scalar_h(3)
+        r_scalar_x(3)
+        q_x(2)
+        r_vector(3)
         lap_q(6)
         lap_q(7)
-        step2(0, range(0, 2))
-        r_scalar(3)
-        r_vector(3)
-        q_x(2)
-        nc.vector.tensor_copy(out=bias2[:], in_=bps[:])
+        q_x(3)
+        step2(1, range(2, 4))
+        w_q()
+        q_a(0, 0, 4)
+        r_gpsimd(4)
+        r_vector(4)
+        r_scalar_h(4)
+        r_scalar_x(4)
+        q_x(4)
+        q_a(1, 0, 4)
+        bias_copy()
+        r_gpsimd(5)
+        r_vector(5)
+        r_scalar_h(5)
+        r_scalar_x(5)
 
-        for k in range(NH - 2):
-            step2(k, range(2, 4) if k == 0 else range(4))
-            if k >= 2:
-                step3_all(k - 2)
-            r_scalar(k + 4)
+        for k in range(2, NH - 2):
+            step2(k, range(0, 3))
+            r_scalar_h(k + 4)
+            step2(k, range(3, 4))
+            r_scalar_x(k + 4)
+            step3_all(k - 2)
             r_gpsimd(k + 4)
             q_x(k + 3)
             q_a(k, 0, 4)

@@ -25,8 +25,8 @@ NA = 5
 NO = 3
 NH = 2 * B
 NR = 32
-SR = [16, 16, 4, 4, 8, 8, 16, 16, 16, 16, 16, 16, 16, 16, 16, 16]
-GP0 = 4
+SR = [16, 16, 8, 8, 16, 16, 16, 16, 16, 16, 16, 16, 16, 16, 16, 16]
+GP0 = 6
 
 FLOPS = 2 * B * N * N * F + 2 * B * N * F * DO
 
@@ -38,7 +38,7 @@ def tile_tgcngraphconvolution_pa_t_kernel(tc, x, h, laplacian, weights, biases, 
         hpool = ctx.enter_context(tc.tile_pool(name="hpool", bufs=8))
         lgpool = ctx.enter_context(tc.tile_pool(name="lgpool", bufs=4))
         xpool = ctx.enter_context(tc.tile_pool(name="xpool", bufs=3))
-        xgpool = ctx.enter_context(tc.tile_pool(name="xgpool", bufs=3))
+        xgpool = ctx.enter_context(tc.tile_pool(name="xgpool", bufs=2))
         apool = ctx.enter_context(tc.tile_pool(name="apool", bufs=4))
         opool = ctx.enter_context(tc.tile_pool(name="opool", bufs=6))
         psa = ctx.enter_context(tc.psum_pool(name="psa", bufs=1))
@@ -131,7 +131,7 @@ def tile_tgcngraphconvolution_pa_t_kernel(tc, x, h, laplacian, weights, biases, 
                 )
 
         def bias_copy():
-            nc.vector.tensor_copy(out=bias2[:], in_=bps[:])
+            nc.scalar.copy(out=bias2[:], in_=bps[:])
 
         gw = const.tile([P, 4 * DO], BF16, name="gw", align_bytes=64)
         wcodes = const.tile([P, DO], U32, name="wcodes", align_bytes=64)
@@ -369,51 +369,52 @@ def tile_tgcngraphconvolution_pa_t_kernel(tc, x, h, laplacian, weights, biases, 
         w_regroup()
         lap_t(4, on_s)
         lap_t(5, on_s)
+        r_scalar_h(2)
+        r_scalar_x(2)
         step2(0, range(2, 4))
         lap_q(4)
         r_vector(2)
-        r_scalar_h(2)
-        r_scalar_x(2)
         lap_q(5)
         lap_t(6, on_s)
         lap_t(7, on_s)
         bias_mm()
-        step2(1, range(0, 2))
         r_scalar_h(3)
         r_scalar_x(3)
+        step2(1, range(0, 2))
         q_x(2)
-        r_vector(3)
         lap_q(6)
         lap_q(7)
+        r_vector(3)
         q_x(3)
         step2(1, range(2, 4))
         w_q()
         q_a(0, 0, 4)
-        r_gpsimd(4)
-        r_vector(4)
         r_scalar_h(4)
         r_scalar_x(4)
-        q_x(4)
+        r_vector(4)
         q_a(1, 0, 4)
+        q_x(4)
         bias_copy()
-        r_gpsimd(5)
-        r_vector(5)
         r_scalar_h(5)
         r_scalar_x(5)
+        r_vector(5)
+        r_gpsimd(6)
 
         for k in range(2, NH - 2):
             step2(k, range(0, 3))
             r_scalar_h(k + 4)
             step2(k, range(3, 4))
             r_scalar_x(k + 4)
-            step3_all(k - 2)
-            r_gpsimd(k + 4)
-            q_x(k + 3)
-            q_a(k, 0, 4)
+            if k > 2:
+                q_a(k - 1, 0, 4)
             r_vector(k + 4)
+            q_x(k + 3)
+            r_gpsimd(k + 5)
+            step3_all(k - 2)
 
         k = NH - 2
         step2(k, range(0, 2))
+        q_a(k - 1, 0, 4)
         step3_all(k - 2)
         q_a(k, 0, 2)
         step2(k, range(2, 4))

@@ -24,8 +24,9 @@ MT = 8
 NA = 5
 NO = 3
 NH = 2 * B
-NR = 32
-SR = [16, 16, 8, 8, 16, 16, 16, 16, 16, 16, 16, 16, 16, 16, 16, 16]
+NR = 64
+RS = [16, 16, 8, 8, 16, 16, 16, 16, 16, 16, 16, 16, 16, 16, 16, 16]
+RG = 16
 GP0 = 6
 
 FLOPS = 2 * B * N * N * F + 2 * B * N * F * DO
@@ -60,7 +61,7 @@ def tile_tgcngraphconvolution_pa_t_kernel(tc, x, h, laplacian, weights, biases, 
         h_v = h.rearrange("b (g p j) f -> b g p (j f)", g=G, j=4)
         x_v = x.rearrange("b (g r) c -> (b g) (r c)", g=G)
         lap_v = laplacian.rearrange("(r i) n -> r (i n)", i=MT)
-        w_v = weights.rearrange("(r s i) d c o -> s r i (d c o)", s=2, i=4)
+        w_v = weights.rearrange("(r t) d c o -> r (t d c o)", t=4)
         b_v = biases.rearrange("(a d) o -> a (d o)", a=1)
         out_v = out.rearrange("b (p r) o -> b p (r o)", p=P)
 
@@ -68,7 +69,7 @@ def tile_tgcngraphconvolution_pa_t_kernel(tc, x, h, laplacian, weights, biases, 
         nc.vector.memset(xrow[:].bitcast(F32), 0.0)
         brow = const.tile([P, DO], BF16, name="brow")
         nc.vector.memset(brow[:].bitcast(F32), 0.0)
-        wraw = const.tile([P, 1024], BF16, name="wraw")
+        wraw = const.tile([P, 2048], BF16, name="wraw")
 
         hraws = []
 
@@ -94,8 +95,8 @@ def tile_tgcngraphconvolution_pa_t_kernel(tc, x, h, laplacian, weights, biases, 
         load_lap(3, 4)
         load_lap(4, 6)
         load_lap(6, 8)
-        for s in range(2):
-            nc.sync.dma_start(out=wraw[:, 512 * s : 512 * s + 512], in_=w_v[s])
+        for c in range(2):
+            nc.sync.dma_start(out=wraw[c:P:2, 0 : 2048 - 2 * c], in_=w_v[:, 2 * c : 2048])
         for b in range(1, B):
             load_h(b, 0)
             load_h(b, 1)
@@ -138,12 +139,14 @@ def tile_tgcngraphconvolution_pa_t_kernel(tc, x, h, laplacian, weights, biases, 
         wplane = const.tile([P, DO], U8, name="wplane", align_bytes=64)
 
         def w_regroup():
-            gw_v = gw[:].rearrange("p (d o s c) -> p s d o c", d=P, o=2, s=2)
-            wr = wraw[:].rearrange("p (s d c o) -> p s d o c", s=2, d=P, c=2)
-            for s in range(2):
-                nc.gpsimd.tensor_scalar(
-                    out=gw_v[:, s], in0=wr[:, s], scalar1=1.0, scalar2=0.0, op0=MULT, op1=ADD
-                )
+            nc.gpsimd.tensor_scalar(
+                out=gw[:].rearrange("p (d o t) -> p d o t", o=2, t=4),
+                in0=wraw[:].rearrange("p (t d c o) -> p d c o t", t=4, c=2, o=2)[:, :, 0],
+                scalar1=1.0,
+                scalar2=0.0,
+                op0=MULT,
+                op1=ADD,
+            )
 
         def w_q():
             nc.vector.quantize_mx(out=wcodes[:].bitcast(FP8X4), scales=wplane[:], in_=gw[:])
@@ -163,52 +166,46 @@ def tile_tgcngraphconvolution_pa_t_kernel(tc, x, h, laplacian, weights, biases, 
                 xgt[q] = xgpool.tile([P, F * 4], BF16, tag="xg", name="xg", align_bytes=64)
             return xgt[q]
 
-        def xg_view(q):
-            return xg_tile(q)[:].rearrange("p (s c r i j) -> p s c r i j", s=2, c=2, r=NR, i=4)
+        def xg_view(q, lo, hi):
+            return xg_tile(q)[:].rearrange("p (t r c j) -> p r t c j", t=4, r=NR, c=2)[:, lo:hi]
 
-        def h_view(q, s, lo, hi):
+        def h_view(q, lo, hi):
             b, g = q // G, q % G
-            start = HP * g + PAD - (2 if s == 0 else 0)
-            f0 = 16 * lo + (0 if s == 0 else 6)
+            f0 = 8 * lo - 2
+            start = HP * g + PAD
+            if lo == 0:
+                start, f0 = start - 2, 0
             rows = hraws[b][:, start : start + 4 * H].rearrange("p (j f) -> p j f", j=4)
-            return rows[:, :, f0 : f0 + 16 * (hi - lo) - 8].rearrange(
-                "p j (r i c) -> p c r i j", i=4, c=2
-            )[:, :, 0 : 2 * (hi - lo) - 1 : 2]
+            return rows[:, :, f0 : f0 + 8 * (hi - lo)].rearrange("p j (r t c) -> p r t c j", t=4, c=2)
 
-        def regroup(copy, q, s, lo, hi):
-            if lo < hi:
-                copy(
-                    out=xg_view(q)[:, s, :, lo:hi].rearrange("p c r i j -> p c r j i"),
-                    in_=h_view(q, s, lo, hi).rearrange("p c r i j -> p c r j i"),
-                )
+        def regroup(copy, q, lo, hi):
+            copy(
+                out=xg_view(q, lo, hi).rearrange("p r t c j -> p r t j c"),
+                in_=h_view(q, lo, hi).rearrange("p r t c j -> p r t j c"),
+            )
 
         def r_scalar_x(q):
             if q < NH:
                 b, g = q // G, q % G
                 nc.scalar.copy(
-                    out=xg_view(q)[:, 0, :, 0, 0, :], in_=xv[:, b, g].rearrange("p j c -> p c j")
+                    out=xg_tile(q)[:, 0:8].rearrange("p (c j) -> p c j", c=2),
+                    in_=xv[:, b, g].rearrange("p j c -> p c j"),
                 )
 
         def r_scalar_h(q):
             if q < NH:
-                regroup(nc.scalar.copy, q, 0, 0, SR[q])
+                regroup(nc.scalar.copy, q, 0, RS[q])
 
         def r_vector(q):
             if q < NH:
-                regroup(nc.vector.tensor_copy, q, 0, SR[q], NR)
-                if q < GP0:
-                    regroup(nc.vector.tensor_copy, q, 1, 0, NR)
-                else:
-                    nc.vector.tensor_copy(
-                        out=xg_view(q)[:, 1, 0].rearrange("p r i j -> p r j i"),
-                        in_=h_view(q, 1, 0, NR)[:, 0].rearrange("p r i j -> p r j i"),
-                    )
+                regroup(nc.vector.tensor_copy, q, RS[q] + (RG if q >= GP0 else 0), NR)
 
         def r_gpsimd(q):
             if GP0 <= q < NH:
+                lo, hi = RS[q], RS[q] + RG
                 nc.gpsimd.tensor_scalar(
-                    out=xg_view(q)[:, 1, 1],
-                    in0=h_view(q, 1, 0, NR)[:, 1],
+                    out=xg_view(q, lo, hi),
+                    in0=h_view(q, lo, hi),
                     scalar1=1.0,
                     scalar2=0.0,
                     op0=MULT,

@@ -65,6 +65,8 @@ def tile_tgcngraphconvolution_pa_t_kernel(tc, x, h, laplacian, weights, biases, 
         b_v = biases.rearrange("(a d) o -> a (d o)", a=1)
         out_v = out.rearrange("b (p r) o -> b p (r o)", p=P)
 
+        zeros = const.tile([P, 512], BF16, name="zeros")
+        nc.vector.memset(zeros[:].bitcast(F32), 0.0)
         xrow = const.tile([P, 1024], BF16, name="xrow")
         nc.vector.memset(xrow[:].bitcast(F32), 0.0)
         brow = const.tile([P, DO], BF16, name="brow")
@@ -109,6 +111,13 @@ def tile_tgcngraphconvolution_pa_t_kernel(tc, x, h, laplacian, weights, biases, 
         nc.scalar.copy(out=warmed[:], in_=ones[:, 0:1])
 
         xraw = const.tile([P, B * 16], BF16, name="xraw")
+        bps = o_bank()
+
+        def warm(n):
+            for w in range(n):
+                nc.tensor.matmul(out=bps[:], lhsT=zeros[:, 0:P], rhs=zeros[:], start=True, stop=True)
+
+        warm(5)
         xps = a_bank()
         xw = xrow[:].bitcast(F32).rearrange("q (p j) -> q p j", j=4)
         for j in range(4):
@@ -123,7 +132,6 @@ def tile_tgcngraphconvolution_pa_t_kernel(tc, x, h, laplacian, weights, biases, 
         xv = xraw[:].rearrange("p (b g j c) -> p b g j c", b=B, g=G, j=4)
 
         bias2 = const.tile([P, 512], F32, name="bias2")
-        bps = o_bank()
 
         def bias_mm():
             for s in range(2):
@@ -350,6 +358,7 @@ def tile_tgcngraphconvolution_pa_t_kernel(tc, x, h, laplacian, weights, biases, 
         x_copy()
         r_scalar_x(0)
         lap_t(0, on_s)
+        warm(3)
         q_x(0)
         r_vector(1)
         r_scalar_h(1)
@@ -357,6 +366,7 @@ def tile_tgcngraphconvolution_pa_t_kernel(tc, x, h, laplacian, weights, biases, 
         lap_q(0)
         q_x(1)
         lap_t(1, on_s)
+        warm(1)
         lap_t(2, on_s)
         lap_q(1)
         lap_t(3, on_v)

@@ -9,7 +9,6 @@ U32 = mybir.dt.uint32
 U8 = mybir.dt.uint8
 FP8X4 = mybir.dt.float8_e4m3fn_x4
 ADD = mybir.AluOpType.add
-MULT = mybir.AluOpType.mult
 
 P = 128
 B = 8
@@ -25,9 +24,7 @@ NA = 5
 NO = 3
 NH = 2 * B
 NR = 64
-RS = [16, 16, 8, 8, 16, 16, 16, 16, 16, 16, 16, 16, 16, 16, 16, 16]
-RG = 16
-GP0 = 6
+RS = [16, 16, 8, 8, 16, 16, 20, 20, 20, 20, 20, 20, 20, 20, 20, 20]
 
 FLOPS = 2 * B * N * N * F + 2 * B * N * F * DO
 
@@ -38,8 +35,9 @@ def tile_tgcngraphconvolution_pa_t_kernel(tc, x, h, laplacian, weights, biases, 
         const = ctx.enter_context(tc.tile_pool(name="const", bufs=1))
         hpool = ctx.enter_context(tc.tile_pool(name="hpool", bufs=8))
         lgpool = ctx.enter_context(tc.tile_pool(name="lgpool", bufs=4))
+        lppool = ctx.enter_context(tc.tile_pool(name="lppool", bufs=4))
         xpool = ctx.enter_context(tc.tile_pool(name="xpool", bufs=3))
-        xgpool = ctx.enter_context(tc.tile_pool(name="xgpool", bufs=2))
+        xgpool = ctx.enter_context(tc.tile_pool(name="xgpool", bufs=3))
         apool = ctx.enter_context(tc.tile_pool(name="apool", bufs=4))
         opool = ctx.enter_context(tc.tile_pool(name="opool", bufs=6))
         psa = ctx.enter_context(tc.psum_pool(name="psa", bufs=1))
@@ -90,13 +88,11 @@ def tile_tgcngraphconvolution_pa_t_kernel(tc, x, h, laplacian, weights, biases, 
         load_h(0, 0)
         nc.sync.dma_start(out=xrow[0 : G * B, :], in_=x_v)
         nc.sync.dma_start(out=brow[0:1, :], in_=b_v)
-        load_lap(0, 1)
+        for i in range(4):
+            load_lap(i, i + 1)
         load_h(0, 1)
-        load_lap(1, 2)
-        load_lap(2, 3)
-        load_lap(3, 4)
-        load_lap(4, 6)
-        load_lap(6, 8)
+        for i in range(4, 8):
+            load_lap(i, i + 1)
         for c in range(2):
             nc.sync.dma_start(out=wraw[c:P:2, 0 : 2048 - 2 * c], in_=w_v[:, 2 * c : 2048])
         for b in range(1, B):
@@ -147,13 +143,9 @@ def tile_tgcngraphconvolution_pa_t_kernel(tc, x, h, laplacian, weights, biases, 
         wplane = const.tile([P, DO], U8, name="wplane", align_bytes=64)
 
         def w_regroup():
-            nc.gpsimd.tensor_scalar(
+            nc.vector.tensor_copy(
                 out=gw[:].rearrange("p (d o t) -> p d o t", o=2, t=4),
-                in0=wraw[:].rearrange("p (t d c o) -> p d c o t", t=4, c=2, o=2)[:, :, 0],
-                scalar1=1.0,
-                scalar2=0.0,
-                op0=MULT,
-                op1=ADD,
+                in_=wraw[:].rearrange("p (t d c o) -> p d c o t", t=4, c=2, o=2)[:, :, 0],
             )
 
         def w_q():
@@ -206,43 +198,46 @@ def tile_tgcngraphconvolution_pa_t_kernel(tc, x, h, laplacian, weights, biases, 
 
         def r_vector(q):
             if q < NH:
-                regroup(nc.vector.tensor_copy, q, RS[q] + (RG if q >= GP0 else 0), NR)
+                regroup(nc.vector.tensor_copy, q, RS[q], NR)
 
-        def r_gpsimd(q):
-            if GP0 <= q < NH:
-                lo, hi = RS[q], RS[q] + RG
-                nc.gpsimd.tensor_scalar(
-                    out=xg_view(q, lo, hi),
-                    in0=h_view(q, lo, hi),
-                    scalar1=1.0,
-                    scalar2=0.0,
-                    op0=MULT,
-                    op1=ADD,
-                )
-
-        def q_x(q):
+        def q_x(q, lo=0, hi=4):
             if q < NH:
                 b, g = q // G, q % G
                 xcodes, xplane = x_tiles(b)
+                cs = slice(F * g + P * lo, F * g + P * hi)
                 nc.vector.quantize_mx(
-                    out=xcodes[:, F * g : F * g + F].bitcast(FP8X4),
-                    scales=xplane[:, F * g : F * g + F],
-                    in_=xg_tile(q)[:],
+                    out=xcodes[:, cs].bitcast(FP8X4),
+                    scales=xplane[:, cs],
+                    in_=xg_tile(q)[:, 512 * lo : 512 * hi],
                 )
 
         lcodes = const.tile([P, MT * G * P], U32, name="lcodes", align_bytes=64)
         lplane = const.tile([P, MT * G * P], U8, name="lplane", align_bytes=64)
         lgrps = {}
+        lperms = {}
+
+        def lap_words(i):
+            return lraw[:].bitcast(F32)[:, 512 * i : 512 * i + 512].rearrange(
+                "p (g n u) -> p g u n", g=G, u=2
+            )
+
+        def lap_p(i, copy):
+            lperms[i] = lppool.tile([P, N], BF16, tag="lperm", name="lperm")
+            copy(
+                out=lperms[i][:].bitcast(F32).rearrange("p (g u n) -> p g u n", g=G, u=2),
+                in_=lap_words(i),
+            )
 
         def lap_t(i, copy):
-            lw = lraw[:].bitcast(F32)[:, 512 * i : 512 * i + 512]
+            if i in lperms:
+                lw = lperms[i][:].bitcast(F32).rearrange("p (g u n) -> p g u n", g=G, u=2)
+            else:
+                lw = lap_words(i)
             lps = a_bank()
             for g in range(G):
                 for u in range(2):
                     nc.tensor.transpose(
-                        lps[:, P * (2 * g + u) : P * (2 * g + u) + P],
-                        lw[:, 256 * g + u : 256 * g + 256 : 2],
-                        ident[:],
+                        lps[:, P * (2 * g + u) : P * (2 * g + u) + P], lw[:, g, u], ident[:]
                     )
             lgrp = lgpool.tile([P, N], BF16, tag="lgrp", name="lgrp", align_bytes=64)
             copy(
@@ -358,40 +353,44 @@ def tile_tgcngraphconvolution_pa_t_kernel(tc, x, h, laplacian, weights, biases, 
         x_copy()
         r_scalar_x(0)
         lap_t(0, on_s)
-        warm(3)
         q_x(0)
+        lap_t(1, on_v)
+        warm(2)
+        lap_q(0)
+        lap_q(1)
         r_vector(1)
         r_scalar_h(1)
         r_scalar_x(1)
-        lap_q(0)
-        q_x(1)
-        lap_t(1, on_s)
-        warm(1)
         lap_t(2, on_s)
-        lap_q(1)
-        lap_t(3, on_v)
-        lap_q(2)
-        step2(0, range(0, 2))
-        lap_q(3)
-        w_regroup()
+        lap_t(3, on_s)
+        warm(1)
+        bias_mm()
+        q_x(1, 0, 2)
+        q_x(1, 2, 4)
         lap_t(4, on_s)
-        lap_t(5, on_s)
-        r_scalar_h(2)
-        r_scalar_x(2)
-        step2(0, range(2, 4))
+        lap_q(2)
+        lap_q(3)
+        lap_p(5, on_v)
+        lap_p(6, on_v)
+        lap_p(7, on_v)
+        step2(0, range(0, 3))
         lap_q(4)
-        r_vector(2)
-        lap_q(5)
+        lap_t(5, on_s)
         lap_t(6, on_s)
         lap_t(7, on_s)
-        bias_mm()
+        w_regroup()
+        r_scalar_h(2)
+        r_vector(2)
+        lap_q(5)
         r_scalar_h(3)
+        r_vector(3)
+        r_scalar_x(2)
         r_scalar_x(3)
+        step2(0, range(3, 4))
         step2(1, range(0, 2))
-        q_x(2)
         lap_q(6)
         lap_q(7)
-        r_vector(3)
+        q_x(2)
         q_x(3)
         step2(1, range(2, 4))
         w_q()
@@ -405,7 +404,6 @@ def tile_tgcngraphconvolution_pa_t_kernel(tc, x, h, laplacian, weights, biases, 
         r_scalar_h(5)
         r_scalar_x(5)
         r_vector(5)
-        r_gpsimd(6)
 
         for k in range(2, NH - 2):
             step2(k, range(0, 3))
@@ -416,7 +414,6 @@ def tile_tgcngraphconvolution_pa_t_kernel(tc, x, h, laplacian, weights, biases, 
                 q_a(k - 1, 0, 4)
             r_vector(k + 4)
             q_x(k + 3)
-            r_gpsimd(k + 5)
             step3_all(k - 2)
 
         k = NH - 2

from contextlib import ExitStack

import concourse.mybir as mybir
from concourse.masks import make_identity

BF16 = mybir.dt.bfloat16
F32 = mybir.dt.float32
U32 = mybir.dt.uint32
U8 = mybir.dt.uint8
FP8X4 = mybir.dt.float8_e4m3fn_x4
ADD = mybir.AluOpType.add

P = 128
B = 8
N = 1024
F = 512
H = 510
DO = 256
G = 2
PAD = 16
HP = PAD + 2048
MT = 8
NA = 5
NO = 3
NH = 2 * B
NR = 64
RS = [16, 16, 8, 8, 16, 16, 20, 20, 20, 20, 20, 20, 20, 20, 20, 20]

FLOPS = 2 * B * N * N * F + 2 * B * N * F * DO


def tile_tgcngraphconvolution_pa_t_kernel(tc, x, h, laplacian, weights, biases, out):
    nc = tc.nc
    with ExitStack() as ctx:
        const = ctx.enter_context(tc.tile_pool(name="const", bufs=1))
        hpool = ctx.enter_context(tc.tile_pool(name="hpool", bufs=8))
        lgpool = ctx.enter_context(tc.tile_pool(name="lgpool", bufs=4))
        lppool = ctx.enter_context(tc.tile_pool(name="lppool", bufs=4))
        xpool = ctx.enter_context(tc.tile_pool(name="xpool", bufs=3))
        xgpool = ctx.enter_context(tc.tile_pool(name="xgpool", bufs=3))
        apool = ctx.enter_context(tc.tile_pool(name="apool", bufs=4))
        opool = ctx.enter_context(tc.tile_pool(name="opool", bufs=6))
        psa = ctx.enter_context(tc.psum_pool(name="psa", bufs=1))
        pso = ctx.enter_context(tc.psum_pool(name="pso", bufs=1))
        ctx.enter_context(tc.manual_schedule())

        count = {"a": 0, "o": 0}

        def a_bank():
            n = count["a"]
            count["a"] = n + 1
            return psa.tile([P, 512], F32, tag="a%d" % (n % NA), name="a%d" % (n % NA))

        def o_bank():
            n = count["o"]
            count["o"] = n + 1
            return pso.tile([P, 512], F32, tag="o%d" % (n % NO), name="o%d" % (n % NO))

        h_v = h.rearrange("b (g p j) f -> b g p (j f)", g=G, j=4)
        x_v = x.rearrange("b (g r) c -> (b g) (r c)", g=G)
        lap_v = laplacian.rearrange("(r i) n -> r (i n)", i=MT)
        w_v = weights.rearrange("(r t) d c o -> r (t d c o)", t=4)
        b_v = biases.rearrange("(a d) o -> a (d o)", a=1)
        out_v = out.rearrange("b (p r) o -> b p (r o)", p=P)

        zeros = const.tile([P, 512], BF16, name="zeros")
        nc.vector.memset(zeros[:].bitcast(F32), 0.0)
        xrow = const.tile([P, 1024], BF16, name="xrow")
        nc.vector.memset(xrow[:].bitcast(F32), 0.0)
        brow = const.tile([P, DO], BF16, name="brow")
        nc.vector.memset(brow[:].bitcast(F32), 0.0)
        wraw = const.tile([P, 2048], BF16, name="wraw")

        hraws = []

        def load_h(b, g):
            if g == 0:
                hraws.append(hpool.tile([P, G * HP], BF16, tag="hraw", name="hraw"))
            hraw = hraws[b]
            nc.gpsimd.memset(hraw[:, HP * g : HP * g + PAD], 0.0)
            nc.sync.dma_start(out=hraw[:, HP * g + PAD : HP * g + PAD + 4 * H], in_=h_v[b][g])

        def load_lap(lo, hi):
            nc.sync.dma_start(out=lraw[:, N * lo : N * hi], in_=lap_v[:, N * lo : N * hi])

        lraw = const.tile([P, MT * N], BF16, name="lraw")

        load_h(0, 0)
        nc.sync.dma_start(out=xrow[0 : G * B, :], in_=x_v)
        nc.sync.dma_start(out=brow[0:1, :], in_=b_v)
        for i in range(4):
            load_lap(i, i + 1)
        load_h(0, 1)
        for i in range(4, 8):
            load_lap(i, i + 1)
        for c in range(2):
            nc.sync.dma_start(out=wraw[c:P:2, 0 : 2048 - 2 * c], in_=w_v[:, 2 * c : 2048])
        for b in range(1, B):
            load_h(b, 0)
            load_h(b, 1)

        ident = const.tile([P, P], F32, name="ident")
        make_identity(nc, ident[:])
        ones = const.tile([P, P], BF16, name="ones")
        nc.vector.memset(ones[:], 1.0)
        warmed = const.tile([P, 1], BF16, name="warmed")
        nc.scalar.copy(out=warmed[:], in_=ones[:, 0:1])

        xraw = const.tile([P, B * 16], BF16, name="xraw")
        bps = o_bank()

        def warm(n):
            for w in range(n):
                nc.tensor.matmul(out=bps[:], lhsT=zeros[:, 0:P], rhs=zeros[:], start=True, stop=True)

        warm(5)
        xps = a_bank()
        xw = xrow[:].bitcast(F32).rearrange("q (p j) -> q p j", j=4)
        for j in range(4):
            nc.tensor.transpose(xps[:, P * j : P * j + P], xw[:, :, j], ident[:])

        def x_copy():
            nc.scalar.copy(
                out=xraw[:].bitcast(F32).rearrange("p (q j) -> p q j", j=4),
                in_=xps[:].rearrange("p (j q) -> p q j", j=4)[:, 0 : G * B, :],
            )

        xv = xraw[:].rearrange("p (b g j c) -> p b g j c", b=B, g=G, j=4)

        bias2 = const.tile([P, 512], F32, name="bias2")

        def bias_mm():
            for s in range(2):
                nc.tensor.matmul(
                    out=bps[:, DO * s : DO * s + DO], lhsT=ones[:], rhs=brow[:], start=True, stop=True
                )

        def bias_copy():
            nc.scalar.copy(out=bias2[:], in_=bps[:])

        gw = const.tile([P, 4 * DO], BF16, name="gw", align_bytes=64)
        wcodes = const.tile([P, DO], U32, name="wcodes", align_bytes=64)
        wplane = const.tile([P, DO], U8, name="wplane", align_bytes=64)

        def w_regroup():
            nc.vector.tensor_copy(
                out=gw[:].rearrange("p (d o t) -> p d o t", o=2, t=4),
                in_=wraw[:].rearrange("p (t d c o) -> p d c o t", t=4, c=2, o=2)[:, :, 0],
            )

        def w_q():
            nc.vector.quantize_mx(out=wcodes[:].bitcast(FP8X4), scales=wplane[:], in_=gw[:])

        xt = {}
        xgt = {}

        def x_tiles(b):
            if b not in xt:
                xcodes = xpool.tile([P, G * F], U32, tag="xcodes", name="xcodes", align_bytes=64)
                xplane = xpool.tile([P, G * F], U8, tag="xplane", name="xplane", align_bytes=64)
                xt[b] = (xcodes, xplane)
            return xt[b]

        def xg_tile(q):
            if q not in xgt:
                xgt[q] = xgpool.tile([P, F * 4], BF16, tag="xg", name="xg", align_bytes=64)
            return xgt[q]

        def xg_view(q, lo, hi):
            return xg_tile(q)[:].rearrange("p (t r c j) -> p r t c j", t=4, r=NR, c=2)[:, lo:hi]

        def h_view(q, lo, hi):
            b, g = q // G, q % G
            f0 = 8 * lo - 2
            start = HP * g + PAD
            if lo == 0:
                start, f0 = start - 2, 0
            rows = hraws[b][:, start : start + 4 * H].rearrange("p (j f) -> p j f", j=4)
            return rows[:, :, f0 : f0 + 8 * (hi - lo)].rearrange("p j (r t c) -> p r t c j", t=4, c=2)

        def regroup(copy, q, lo, hi):
            copy(
                out=xg_view(q, lo, hi).rearrange("p r t c j -> p r t j c"),
                in_=h_view(q, lo, hi).rearrange("p r t c j -> p r t j c"),
            )

        def r_scalar_x(q):
            if q < NH:
                b, g = q // G, q % G
                nc.scalar.copy(
                    out=xg_tile(q)[:, 0:8].rearrange("p (c j) -> p c j", c=2),
                    in_=xv[:, b, g].rearrange("p j c -> p c j"),
                )

        def r_scalar_h(q):
            if q < NH:
                regroup(nc.scalar.copy, q, 0, RS[q])

        def r_vector(q):
            if q < NH:
                regroup(nc.vector.tensor_copy, q, RS[q], NR)

        def q_x(q, lo=0, hi=4):
            if q < NH:
                b, g = q // G, q % G
                xcodes, xplane = x_tiles(b)
                cs = slice(F * g + P * lo, F * g + P * hi)
                nc.vector.quantize_mx(
                    out=xcodes[:, cs].bitcast(FP8X4),
                    scales=xplane[:, cs],
                    in_=xg_tile(q)[:, 512 * lo : 512 * hi],
                )

        lcodes = const.tile([P, MT * G * P], U32, name="lcodes", align_bytes=64)
        lplane = const.tile([P, MT * G * P], U8, name="lplane", align_bytes=64)
        lgrps = {}
        lperms = {}

        def lap_words(i):
            return lraw[:].bitcast(F32)[:, 512 * i : 512 * i + 512].rearrange(
                "p (g n u) -> p g u n", g=G, u=2
            )

        def lap_p(i, copy):
            lperms[i] = lppool.tile([P, N], BF16, tag="lperm", name="lperm")
            copy(
                out=lperms[i][:].bitcast(F32).rearrange("p (g u n) -> p g u n", g=G, u=2),
                in_=lap_words(i),
            )

        def lap_t(i, copy):
            if i in lperms:
                lw = lperms[i][:].bitcast(F32).rearrange("p (g u n) -> p g u n", g=G, u=2)
            else:
                lw = lap_words(i)
            lps = a_bank()
            for g in range(G):
                for u in range(2):
                    nc.tensor.transpose(
                        lps[:, P * (2 * g + u) : P * (2 * g + u) + P], lw[:, g, u], ident[:]
                    )
            lgrp = lgpool.tile([P, N], BF16, tag="lgrp", name="lgrp", align_bytes=64)
            copy(
                out=lgrp[:].bitcast(F32).rearrange("p (g m u) -> p g m u", g=G, u=2),
                in_=lps[:].rearrange("p (g u m) -> p g m u", g=G, u=2),
            )
            lgrps[i] = lgrp

        def lap_q(i):
            nc.vector.quantize_mx(
                out=lcodes[:, 256 * i : 256 * i + 256].bitcast(FP8X4),
                scales=lplane[:, 256 * i : 256 * i + 256],
                in_=lgrps[i][:],
            )

        at = {}

        def step2(k, tiles):
            b, hf = k // 2, k % 2
            xcodes, xplane = x_tiles(b)
            if k not in at:
                ag = apool.tile([P, 2048], BF16, tag="ag", name="ag", align_bytes=64)
                acodes = apool.tile([P, 512], U32, tag="acodes", name="acodes", align_bytes=64)
                aplane = apool.tile([P, 512], U8, tag="aplane", name="aplane", align_bytes=64)
                osb = opool.tile([P, 1024], F32, tag="osb", name="osb")
                at[k] = (ag, acodes, aplane, osb)
            ag = at[k][0]
            for ii in tiles:
                i = 4 * hf + ii
                aps = a_bank()
                for t in range(4):
                    for g in range(G):
                        xs = slice(F * g + P * t, F * g + P * t + P)
                        ls = slice(256 * i + P * g, 256 * i + P * g + P)
                        nc.tensor.matmul_mx(
                            out=aps[:, P * t : P * t + P],
                            lhsT=xcodes[:, xs].bitcast(FP8X4),
                            lhsT_scale=xplane[:, xs],
                            rhs=lcodes[:, ls].bitcast(FP8X4),
                            rhs_scale=lplane[:, ls],
                            start=(g == 0),
                            stop=(g == G - 1),
                        )
                nc.scalar.copy(
                    out=ag[:, 512 * ii : 512 * ii + 512].rearrange("p (m t) -> p m t", t=4),
                    in_=aps[:].rearrange("p (t m) -> p m t", t=4),
                )

        def q_a(k, lo, hi):
            ag, acodes, aplane = at[k][0:3]
            nc.vector.quantize_mx(
                out=acodes[:, P * lo : P * hi].bitcast(FP8X4),
                scales=aplane[:, P * lo : P * hi],
                in_=ag[:, 512 * lo : 512 * hi],
            )

        def step3(k, pr):
            acodes, aplane, osb = at[k][1:]
            ops = o_bank()
            for s in range(2):
                cs = slice(P * (2 * pr + s), P * (2 * pr + s) + P)
                nc.tensor.matmul_mx(
                    out=ops[:, DO * s : DO * s + DO],
                    lhsT=acodes[:, cs].bitcast(FP8X4),
                    lhsT_scale=aplane[:, cs],
                    rhs=wcodes[:].bitcast(FP8X4),
                    rhs_scale=wplane[:],
                    start=True,
                    stop=True,
                )
            nc.vector.tensor_tensor(
                out=osb[:, 512 * pr : 512 * pr + 512], in0=ops[:], in1=bias2[:], op=ADD
            )

        def store(k, lo, hi):
            b, hf = k // 2, k % 2
            nc.sync.dma_start(
                out=out_v[b][:, 1024 * hf + 512 * lo : 1024 * hf + 512 * hi],
                in_=at[k][3][:, 512 * lo : 512 * hi],
            )

        def step3_tile(k, t):
            b, hf = k // 2, k % 2
            acodes, aplane, osb = at[k][1:]
            ops = o_bank()
            cs = slice(P * t, P * t + P)
            nc.tensor.matmul_mx(
                out=ops[:, 0:DO],
                lhsT=acodes[:, cs].bitcast(FP8X4),
                lhsT_scale=aplane[:, cs],
                rhs=wcodes[:].bitcast(FP8X4),
                rhs_scale=wplane[:],
                start=True,
                stop=True,
            )
            nc.vector.tensor_tensor(
                out=osb[:, DO * t : DO * t + DO], in0=ops[:, 0:DO], in1=bias2[:, 0:DO], op=ADD
            )
            nc.sync.dma_start(
                out=out_v[b][:, 1024 * hf + DO * t : 1024 * hf + DO * t + DO],
                in_=osb[:, DO * t : DO * t + DO],
            )

        def step3_all(k):
            step3(k, 0)
            step3(k, 1)
            store(k, 0, 2)

        on_s, on_v = nc.scalar.copy, nc.vector.tensor_copy

        r_vector(0)
        r_scalar_h(0)
        x_copy()
        r_scalar_x(0)
        lap_t(0, on_s)
        q_x(0)
        lap_t(1, on_v)
        warm(2)
        lap_q(0)
        lap_q(1)
        r_vector(1)
        r_scalar_h(1)
        r_scalar_x(1)
        lap_t(2, on_s)
        lap_t(3, on_s)
        warm(1)
        bias_mm()
        q_x(1, 0, 2)
        q_x(1, 2, 4)
        lap_t(4, on_s)
        lap_q(2)
        lap_q(3)
        lap_p(5, on_v)
        lap_p(6, on_v)
        lap_p(7, on_v)
        step2(0, range(0, 3))
        lap_q(4)
        lap_t(5, on_s)
        lap_t(6, on_s)
        lap_t(7, on_s)
        w_regroup()
        r_scalar_h(2)
        r_vector(2)
        lap_q(5)
        r_scalar_h(3)
        r_vector(3)
        r_scalar_x(2)
        r_scalar_x(3)
        step2(0, range(3, 4))
        step2(1, range(0, 2))
        lap_q(6)
        lap_q(7)
        q_x(2)
        q_x(3)
        step2(1, range(2, 4))
        w_q()
        q_a(0, 0, 4)
        r_scalar_h(4)
        r_scalar_x(4)
        r_vector(4)
        q_a(1, 0, 4)
        q_x(4)
        bias_copy()
        r_scalar_h(5)
        r_scalar_x(5)
        r_vector(5)

        for k in range(2, NH - 2):
            step2(k, range(0, 3))
            r_scalar_h(k + 4)
            step2(k, range(3, 4))
            r_scalar_x(k + 4)
            if k > 2:
                q_a(k - 1, 0, 4)
            r_vector(k + 4)
            q_x(k + 3)
            step3_all(k - 2)

        k = NH - 2
        step2(k, range(0, 2))
        q_a(k - 1, 0, 4)
        step3_all(k - 2)
        q_a(k, 0, 2)
        step2(k, range(2, 4))
        step3_all(k - 1)
        q_a(k, 2, 4)

        k = NH - 1
        step2(k, range(0, 2))
        step3(k - 1, 0)
        q_a(k, 0, 2)
        step2(k, range(2, 3))
        step3(k - 1, 1)
        store(k - 1, 0, 2)
        q_a(k, 2, 3)
        step2(k, range(3, 4))
        step3(k, 0)
        store(k, 0, 1)
        q_a(k, 3, 4)
        step3_tile(k, 2)
        step3_tile(k, 3)
